import numpy as np
import ml_dtypes


def mxq(x, axis, fmt="e4m3"):
    dtype, down = {"e4m3": (ml_dtypes.float8_e4m3fn, 7), "e5m2": (ml_dtypes.float8_e5m2, 14)}[fmt]
    v = np.moveaxis(np.asarray(x, np.float32).astype(ml_dtypes.bfloat16).astype(np.float64), axis, -1)
    blocks = v.reshape(v.shape[:-1] + (-1, 32))
    amax = np.abs(blocks).max(-1, keepdims=True)
    byte = np.maximum(np.where(amax > 0, np.frexp(amax)[1] - 1 + 127, 0) - down, 1)
    scale = np.exp2(byte - 127.0)
    codes = (blocks / scale).astype(np.float32).astype(dtype).astype(np.float64)
    return np.moveaxis((codes * scale).reshape(v.shape), -1, axis)


WIDE = False


def mx_kscale(k):
    if not WIDE:
        return np.ones(k)
    levels = np.array([10, -10, 5, -5, 0])
    a = np.random.permutation(np.resize(levels, k // 512 * 4)).reshape(k // 512, 4)
    idx = np.arange(k)
    return np.exp2(a[idx // 512, idx % 128 // 32])


BF16 = ml_dtypes.bfloat16


def bf(x):
    return np.asarray(x, np.float32).astype(BF16)


def f64(x):
    return np.asarray(x).astype(np.float64)


B, L, F, A = 256, 3, 2048, 768


def setup_inputs():
    s = mx_kscale(F)
    return {"x": bf(np.random.standard_normal((B, L, F)) * s),
            "W": bf(np.random.standard_normal((L, L, F, A)) * 0.016 / s[:, None])}


def reference(x, W):
    n = W.shape[0]
    mask = np.tril(np.ones((n, n)))
    Wm = mxq(f64(W), 2, "e4m3") * mask[:, :, None, None]
    xq = mxq(f64(x), 2, "e4m3")
    rows = []
    for i in range(n):
        acc = 0.0
        for j in range(i + 1):
            acc = acc + (xq[:, j, :] @ Wm[i, j])
        rows.append(acc)
    return np.stack(rows, axis=1)

@@ -1,0 +1,199 @@
+from contextlib import ExitStack
+
+import concourse.mybir as mybir
+from concourse.masks import make_identity
+
+FP8X4 = mybir.dt.float8_e4m3fn_x4
+BF16 = mybir.dt.bfloat16
+F32 = mybir.dt.float32
+U32 = mybir.dt.uint32
+U8 = mybir.dt.uint8
+
+P = 128
+B, L, F, A = 256, 3, 2048, 768
+PACK = 4
+K_PASS = P * PACK
+G = F // K_PASS
+MT = B // P
+
+FLOPS = 2 * B * F * A * 6
+BYTES = B * L * F * 2 + 6 * F * A * 2 + B * L * A * 4
+
+RAW_BUFS = 22
+CV = 376
+N_SLICES = ((0, 512), (512, 256))
+
+
+def tile_decoder_kernel(tc, x, W, out):
+    nc = tc.nc
+    with ExitStack() as ctx:
+        const = ctx.enter_context(tc.tile_pool(name="const", bufs=1))
+        rawp = ctx.enter_context(tc.tile_pool(name="rawp", bufs=RAW_BUFS))
+        xgp = ctx.enter_context(tc.tile_pool(name="xgp", bufs=2))
+        grpp = ctx.enter_context(tc.tile_pool(name="grpp", bufs=3))
+        codep = ctx.enter_context(tc.tile_pool(name="codep", bufs=4))
+        stagep = ctx.enter_context(tc.tile_pool(name="stagep", bufs=1))
+        psum = ctx.enter_context(tc.psum_pool(name="psum", bufs=1))
+        ctx.enter_context(tc.manual_schedule())
+
+        ident = const.tile([P, P], F32, name="ident")
+        make_identity(nc, ident[:])
+
+        x_codes = const.tile([P, L, G * MT * P], U32, name="x_codes", align_bytes=64)
+        x_scales = const.tile([P, L, G * MT * P], U8, name="x_scales", align_bytes=64)
+
+        chunks = [(i, j, g) for i in range(L) for j in range(i + 1) for g in range(G)]
+        items = []
+        for c, ch in enumerate(chunks):
+            if c < L:
+                items.append(("x", c, 0))
+                items.append(("x", c, 1))
+            items.append(("w", c, 0))
+        raw_of = {}
+        n_loaded = [0]
+
+        def load_next():
+            n = n_loaded[0]
+            if n >= len(items):
+                return
+            n_loaded[0] = n + 1
+            kind, a0, a1 = items[n]
+            if kind == "x":
+                t = rawp.tile([P, F], BF16, name="xraw%d_%d" % (a0, a1), tag="raw", align_bytes=64)
+                nc.sync.dma_start(out=t[:], in_=x[a1 * P : (a1 + 1) * P, a0, :])
+            else:
+                i, j, g = chunks[a0]
+                t = rawp.tile([P, PACK, A], BF16, name="wraw%d" % a0, tag="raw", align_bytes=64)
+                nc.sync.dma_start(
+                    out=t[:],
+                    in_=W[i, j, g * K_PASS : (g + 1) * K_PASS, :].rearrange("(p t) a -> p t a", t=PACK),
+                )
+            raw_of[(kind, a0, a1)] = t
+
+        for n in range(RAW_BUFS):
+            load_next()
+
+        xt_of = {}
+        xg_of = {}
+
+        def xt(j):
+            for g in range(G):
+                bank = psum.tile([P, MT, 2, P], F32, name="xt%d_%d" % (j, g), tag="bk%d" % (4 + g))
+                for m in range(MT):
+                    words = raw_of[("x", j, m)][:].bitcast(F32).rearrange(
+                        "p (g q u) -> p g u q", g=G, q=P, u=2
+                    )
+                    for u in range(2):
+                        nc.tensor.transpose(bank[:, m, u, :], words[:, g, u, :], ident[:])
+                xt_of[(j, g)] = bank
+
+        def xe(j):
+            xg = xgp.tile([P, G * MT * P * PACK], BF16, name="xg%d" % j, tag="xg", align_bytes=64)
+            xg_of[j] = xg
+            view = xg[:].bitcast(F32).rearrange("p (g m b u) -> p g m b u", g=G, m=MT, b=P, u=2)
+            for g in range(G):
+                src = xt_of[(j, g)][:].rearrange("p m u b -> p m b u")
+                if g == 0:
+                    nc.vector.tensor_copy(out=view[:, g], in_=src)
+                else:
+                    nc.scalar.copy(out=view[:, g], in_=src)
+            load_next()
+            load_next()
+
+        def xq(j):
+            nc.vector.quantize_mx(
+                out=x_codes[:, j, :].bitcast(FP8X4), scales=x_scales[:, j, :], in_=xg_of[j][:]
+            )
+
+        grp_of = {}
+        code_of = {}
+        acc_of = {}
+
+        def rg(c):
+            raw = raw_of[("w", c, 0)]
+            grp = grpp.tile([P, A, PACK], BF16, name="grp%d" % c, tag="grp", align_bytes=64)
+            grp_of[c] = grp
+            nc.vector.tensor_copy(
+                out=grp[:, 0:CV, :].rearrange("p (c i) t -> p c t i", i=4),
+                in_=raw[:, :, 0:CV].rearrange("p t (c i) -> p c t i", i=4),
+            )
+            nc.scalar.copy(
+                out=grp[:, CV:A, :].rearrange("p (c i) t -> p c t i", i=4),
+                in_=raw[:, :, CV:A].rearrange("p t (c i) -> p c t i", i=4),
+            )
+            load_next()
+
+        def qz(c):
+            codes = codep.tile([P, A], U32, name="wc%d" % c, tag="wc", align_bytes=64)
+            scales = codep.tile([P, A], U8, name="ws%d" % c, tag="ws", align_bytes=64)
+            code_of[c] = (codes, scales)
+            flat = grp_of[c][:].rearrange("p a t -> p (a t)")
+            for n0, nw in N_SLICES:
+                nc.vector.quantize_mx(
+                    out=codes[:, n0 : n0 + nw].bitcast(FP8X4),
+                    scales=scales[:, n0 : n0 + nw],
+                    in_=flat[:, n0 * PACK : (n0 + nw) * PACK],
+                )
+
+        def mm(c):
+            i, j, g = chunks[c]
+            codes, scales = code_of[c]
+            first = j == 0 and g == 0
+            last = j == i and g == G - 1
+            for m in range(MT):
+                for s, (n0, nw) in enumerate(N_SLICES):
+                    if first:
+                        acc_of[(i, m, s)] = psum.tile(
+                            [P, nw], F32, name="acc%d_%d_%d" % (i, m, s), tag="bk%d" % (4 * (i % 2) + 2 * m + s)
+                        )
+                    col = (g * MT + m) * P
+                    nc.tensor.matmul_mx(
+                        out=acc_of[(i, m, s)][:],
+                        lhsT=x_codes[:, j, col : col + P].bitcast(FP8X4),
+                        lhsT_scale=x_scales[:, j, col : col + P],
+                        rhs=codes[:, n0 : n0 + nw].bitcast(FP8X4),
+                        rhs_scale=scales[:, n0 : n0 + nw],
+                        start=first,
+                        stop=last,
+                    )
+
+        def oe(i):
+            for m in range(MT):
+                stage = stagep.tile([P, A], F32, name="st%d_%d" % (i, m))
+                for s, (n0, nw) in enumerate(N_SLICES):
+                    if m == 0:
+                        nc.vector.tensor_copy(out=stage[:, n0 : n0 + nw], in_=acc_of[(i, m, s)][:])
+                    else:
+                        nc.scalar.copy(out=stage[:, n0 : n0 + nw], in_=acc_of[(i, m, s)][:])
+                nc.sync.dma_start(out=out[m * P : (m + 1) * P, i, :], in_=stage[:])
+
+        xt(0)
+        xe(0)
+        rg(0)
+        xq(0)
+        xt(1)
+        rg(1)
+        qz(0)
+        mm(0)
+        xe(1)
+        xt(2)
+        rg(2)
+        xq(1)
+        qz(1)
+        mm(1)
+        xe(2)
+        rg(3)
+        xq(2)
+        qz(2)
+        mm(2)
+        for c in range(4, len(chunks)):
+            rg(c)
+            qz(c - 1)
+            mm(c - 1)
+            if c == 5:
+                oe(0)
+            if c == 13:
+                oe(1)
+        qz(len(chunks) - 1)
+        mm(len(chunks) - 1)
+        oe(2)

@@ -19,9 +19,12 @@ MT = B // P
 FLOPS = 2 * B * F * A * 6
 BYTES = B * L * F * 2 + 6 * F * A * 2 + B * L * A * 4
 
-RAW_BUFS = 22
-CV = 376
+RAW_BUFS = 20
 N_SLICES = ((0, 512), (512, 256))
+PE_FROM = 5
+PE_COLS = 192
+CV_HEAD = 376
+CV_MAIN = 312
 
 
 def tile_decoder_kernel(tc, x, W, out):
@@ -29,26 +32,24 @@ def tile_decoder_kernel(tc, x, W, out):
     with ExitStack() as ctx:
         const = ctx.enter_context(tc.tile_pool(name="const", bufs=1))
         rawp = ctx.enter_context(tc.tile_pool(name="rawp", bufs=RAW_BUFS))
-        xgp = ctx.enter_context(tc.tile_pool(name="xgp", bufs=2))
-        grpp = ctx.enter_context(tc.tile_pool(name="grpp", bufs=3))
-        codep = ctx.enter_context(tc.tile_pool(name="codep", bufs=4))
+        xgp = ctx.enter_context(tc.tile_pool(name="xgp", bufs=3))
+        grpp = ctx.enter_context(tc.tile_pool(name="grpp", bufs=4))
+        codep = ctx.enter_context(tc.tile_pool(name="codep", bufs=6))
         stagep = ctx.enter_context(tc.tile_pool(name="stagep", bufs=1))
         psum = ctx.enter_context(tc.psum_pool(name="psum", bufs=1))
         ctx.enter_context(tc.manual_schedule())
 
         ident = const.tile([P, P], F32, name="ident")
         make_identity(nc, ident[:])
+        ident_bf = const.tile([P, P], BF16, name="ident_bf")
+        make_identity(nc, ident_bf[:])
 
         x_codes = const.tile([P, L, G * MT * P], U32, name="x_codes", align_bytes=64)
         x_scales = const.tile([P, L, G * MT * P], U8, name="x_scales", align_bytes=64)
 
         chunks = [(i, j, g) for i in range(L) for j in range(i + 1) for g in range(G)]
-        items = []
-        for c, ch in enumerate(chunks):
-            if c < L:
-                items.append(("x", c, 0))
-                items.append(("x", c, 1))
-            items.append(("w", c, 0))
+        NCH = len(chunks)
+        items = [("x", j, m) for j in range(L) for m in range(MT)] + [("w", c, 0) for c in range(NCH)]
         raw_of = {}
         n_loaded = [0]
 
@@ -77,8 +78,9 @@ def tile_decoder_kernel(tc, x, W, out):
         xg_of = {}
 
         def xt(j):
+            base = 0 if j == 1 else 4
             for g in range(G):
-                bank = psum.tile([P, MT, 2, P], F32, name="xt%d_%d" % (j, g), tag="bk%d" % (4 + g))
+                bank = psum.tile([P, MT, 2, P], F32, name="xt%d_%d" % (j, g), tag="bk%d" % (base + g))
                 for m in range(MT):
                     words = raw_of[("x", j, m)][:].bitcast(F32).rearrange(
                         "p (g q u) -> p g u q", g=G, q=P, u=2
@@ -108,19 +110,43 @@ def tile_decoder_kernel(tc, x, W, out):
         grp_of = {}
         code_of = {}
         acc_of = {}
+        pg_of = {}
+
+        def pe_cols(c):
+            return PE_COLS if c >= PE_FROM else 0
+
+        def im(c):
+            if c >= NCH or pe_cols(c) == 0:
+                return
+            raw = raw_of[("w", c, 0)]
+            pg = psum.tile([P, PE_COLS * PACK], BF16, name="pg%d" % c, tag="bk%d" % (4 + c % 4))
+            pg_of[c] = pg
+            a0 = A - PE_COLS
+            for o0, ow in ((0, 128), (128, 64)):
+                nc.tensor.matmul(
+                    out=pg[:, o0 * PACK : (o0 + ow) * PACK].rearrange("p (a t) -> p t a", t=PACK),
+                    lhsT=ident_bf[:],
+                    rhs=raw[:, :, a0 + o0 : a0 + o0 + ow],
+                    start=True,
+                    stop=True,
+                )
 
         def rg(c):
             raw = raw_of[("w", c, 0)]
             grp = grpp.tile([P, A, PACK], BF16, name="grp%d" % c, tag="grp", align_bytes=64)
             grp_of[c] = grp
+            cv = CV_MAIN if pe_cols(c) else CV_HEAD
+            cs = A - pe_cols(c)
             nc.vector.tensor_copy(
-                out=grp[:, 0:CV, :].rearrange("p (c i) t -> p c t i", i=4),
-                in_=raw[:, :, 0:CV].rearrange("p t (c i) -> p c t i", i=4),
+                out=grp[:, 0:cv, :].rearrange("p (c i) t -> p c t i", i=4),
+                in_=raw[:, :, 0:cv].rearrange("p t (c i) -> p c t i", i=4),
             )
             nc.scalar.copy(
-                out=grp[:, CV:A, :].rearrange("p (c i) t -> p c t i", i=4),
-                in_=raw[:, :, CV:A].rearrange("p t (c i) -> p c t i", i=4),
+                out=grp[:, cv:cs, :].rearrange("p (c i) t -> p c t i", i=4),
+                in_=raw[:, :, cv:cs].rearrange("p t (c i) -> p c t i", i=4),
             )
+            if pe_cols(c):
+                nc.scalar.copy(out=grp[:, cs:A, :].rearrange("p a t -> p (a t)"), in_=pg_of[c][:])
             load_next()
 
         def qz(c):
@@ -140,60 +166,56 @@ def tile_decoder_kernel(tc, x, W, out):
             codes, scales = code_of[c]
             first = j == 0 and g == 0
             last = j == i and g == G - 1
-            for m in range(MT):
-                for s, (n0, nw) in enumerate(N_SLICES):
-                    if first:
-                        acc_of[(i, m, s)] = psum.tile(
-                            [P, nw], F32, name="acc%d_%d_%d" % (i, m, s), tag="bk%d" % (4 * (i % 2) + 2 * m + s)
-                        )
-                    col = (g * MT + m) * P
-                    nc.tensor.matmul_mx(
-                        out=acc_of[(i, m, s)][:],
-                        lhsT=x_codes[:, j, col : col + P].bitcast(FP8X4),
-                        lhsT_scale=x_scales[:, j, col : col + P],
-                        rhs=codes[:, n0 : n0 + nw].bitcast(FP8X4),
-                        rhs_scale=scales[:, n0 : n0 + nw],
-                        start=first,
-                        stop=last,
+            if c == NCH - 1:
+                seq = [(0, 0), (1, 0), (0, 1), (1, 1)]
+            else:
+                seq = [(0, 0), (0, 1), (1, 0), (1, 1)]
+            for m, s in seq:
+                n0, nw = N_SLICES[s]
+                if first:
+                    acc_of[(i, m, s)] = psum.tile(
+                        [P, nw], F32, name="acc%d_%d_%d" % (i, m, s), tag="bk%d" % (2 * m + s)
                     )
+                col = (g * MT + m) * P
+                nc.tensor.matmul_mx(
+                    out=acc_of[(i, m, s)][:],
+                    lhsT=x_codes[:, j, col : col + P].bitcast(FP8X4),
+                    lhsT_scale=x_scales[:, j, col : col + P],
+                    rhs=codes[:, n0 : n0 + nw].bitcast(FP8X4),
+                    rhs_scale=scales[:, n0 : n0 + nw],
+                    start=first,
+                    stop=last,
+                )
 
         def oe(i):
+            stages = [stagep.tile([P, A], F32, name="st%d_%d" % (i, m)) for m in range(MT)]
+            for s, (n0, nw) in enumerate(N_SLICES):
+                nc.scalar.copy(out=stages[0][:, n0 : n0 + nw], in_=acc_of[(i, 0, s)][:])
+                nc.vector.tensor_copy(out=stages[1][:, n0 : n0 + nw], in_=acc_of[(i, 1, s)][:])
             for m in range(MT):
-                stage = stagep.tile([P, A], F32, name="st%d_%d" % (i, m))
-                for s, (n0, nw) in enumerate(N_SLICES):
-                    if m == 0:
-                        nc.vector.tensor_copy(out=stage[:, n0 : n0 + nw], in_=acc_of[(i, m, s)][:])
-                    else:
-                        nc.scalar.copy(out=stage[:, n0 : n0 + nw], in_=acc_of[(i, m, s)][:])
-                nc.sync.dma_start(out=out[m * P : (m + 1) * P, i, :], in_=stage[:])
+                nc.sync.dma_start(out=out[m * P : (m + 1) * P, i, :], in_=stages[m][:])
 
         xt(0)
-        xe(0)
-        rg(0)
-        xq(0)
         xt(1)
-        rg(1)
-        qz(0)
-        mm(0)
-        xe(1)
+        xe(0)
         xt(2)
-        rg(2)
-        xq(1)
-        qz(1)
-        mm(1)
+        xe(1)
+        xq(0)
         xe(2)
-        rg(3)
+        xq(1)
+        im(0)
+        rg(0)
         xq(2)
-        qz(2)
-        mm(2)
-        for c in range(4, len(chunks)):
+        im(1)
+        for c in range(1, NCH):
             rg(c)
             qz(c - 1)
-            mm(c - 1)
+            im(c + 1)
             if c == 5:
                 oe(0)
             if c == 13:
                 oe(1)
-        qz(len(chunks) - 1)
-        mm(len(chunks) - 1)
+            mm(c - 1)
+        qz(NCH - 1)
+        mm(NCH - 1)
         oe(2)

@@ -24,7 +24,7 @@ N_SLICES = ((0, 512), (512, 256))
 PE_FROM = 5
 PE_COLS = 192
 CV_HEAD = 376
-CV_MAIN = 312
+CV_MAIN = 328
 
 
 def tile_decoder_kernel(tc, x, W, out):

@@ -24,7 +24,9 @@ N_SLICES = ((0, 512), (512, 256))
 PE_FROM = 5
 PE_COLS = 192
 CV_HEAD = 376
-CV_MAIN = 328
+CV_MAIN = 312
+CV_AFTER_OUT = 448
+OUT_AT = {5: 0, 13: 1}
 
 
 def tile_decoder_kernel(tc, x, W, out):
@@ -44,12 +46,17 @@ def tile_decoder_kernel(tc, x, W, out):
         ident_bf = const.tile([P, P], BF16, name="ident_bf")
         make_identity(nc, ident_bf[:])
 
-        x_codes = const.tile([P, L, G * MT * P], U32, name="x_codes", align_bytes=64)
-        x_scales = const.tile([P, L, G * MT * P], U8, name="x_scales", align_bytes=64)
+        x_codes = const.tile([P, L, MT * G * P], U32, name="x_codes", align_bytes=64)
+        x_scales = const.tile([P, L, MT * G * P], U8, name="x_scales", align_bytes=64)
 
         chunks = [(i, j, g) for i in range(L) for j in range(i + 1) for g in range(G)]
         NCH = len(chunks)
-        items = [("x", j, m) for j in range(L) for m in range(MT)] + [("w", c, 0) for c in range(NCH)]
+        late_x = [(1, 0), (1, 1), (2, 0), (2, 1)]
+        items = [("x", 0, 0), ("x", 0, 1)]
+        for c in range(NCH):
+            items.append(("w", c, 0))
+            if c < len(late_x):
+                items.append(("x",) + late_x[c])
         raw_of = {}
         n_loaded = [0]
 
@@ -76,35 +83,36 @@ def tile_decoder_kernel(tc, x, W, out):
 
         xt_of = {}
         xg_of = {}
+        n_items = [0]
 
-        def xt(j):
-            base = 0 if j == 1 else 4
-            for g in range(G):
-                bank = psum.tile([P, MT, 2, P], F32, name="xt%d_%d" % (j, g), tag="bk%d" % (base + g))
-                for m in range(MT):
-                    words = raw_of[("x", j, m)][:].bitcast(F32).rearrange(
-                        "p (g q u) -> p g u q", g=G, q=P, u=2
-                    )
+        def xt(j, m):
+            base = 4 + 2 * (n_items[0] % 2)
+            n_items[0] += 1
+            words = raw_of[("x", j, m)][:].bitcast(F32).rearrange("p (g q u) -> p g u q", g=G, q=P, u=2)
+            for h in range(2):
+                bank = psum.tile([P, 2, 2, P], F32, name="xt%d_%d_%d" % (j, m, h), tag="bk%d" % (base + h))
+                for g2 in range(2):
                     for u in range(2):
-                        nc.tensor.transpose(bank[:, m, u, :], words[:, g, u, :], ident[:])
-                xt_of[(j, g)] = bank
+                        nc.tensor.transpose(bank[:, g2, u, :], words[:, 2 * h + g2, u, :], ident[:])
+                xt_of[(j, m, h)] = bank
 
-        def xe(j):
-            xg = xgp.tile([P, G * MT * P * PACK], BF16, name="xg%d" % j, tag="xg", align_bytes=64)
-            xg_of[j] = xg
-            view = xg[:].bitcast(F32).rearrange("p (g m b u) -> p g m b u", g=G, m=MT, b=P, u=2)
-            for g in range(G):
-                src = xt_of[(j, g)][:].rearrange("p m u b -> p m b u")
-                if g == 0:
-                    nc.vector.tensor_copy(out=view[:, g], in_=src)
-                else:
-                    nc.scalar.copy(out=view[:, g], in_=src)
-            load_next()
+        def xe(j, m):
+            if m == 0:
+                xg_of[j] = xgp.tile([P, MT * G * P * PACK], BF16, name="xg%d" % j, tag="xg", align_bytes=64)
+            view = xg_of[j][:].bitcast(F32).rearrange("p (m g b u) -> p m g b u", m=MT, g=G, b=P, u=2)
+            for h in range(2):
+                nc.scalar.copy(
+                    out=view[:, m, 2 * h : 2 * h + 2],
+                    in_=xt_of[(j, m, h)][:].rearrange("p g u b -> p g b u"),
+                )
             load_next()
 
-        def xq(j):
+        def xq(j, m):
+            w = G * P
             nc.vector.quantize_mx(
-                out=x_codes[:, j, :].bitcast(FP8X4), scales=x_scales[:, j, :], in_=xg_of[j][:]
+                out=x_codes[:, j, m * w : (m + 1) * w].bitcast(FP8X4),
+                scales=x_scales[:, j, m * w : (m + 1) * w],
+                in_=xg_of[j][:, m * w * PACK : (m + 1) * w * PACK],
             )
 
         grp_of = {}
@@ -114,6 +122,13 @@ def tile_decoder_kernel(tc, x, W, out):
 
         def pe_cols(c):
             return PE_COLS if c >= PE_FROM else 0
+
+        def vector_cols(c):
+            if pe_cols(c) == 0:
+                return CV_HEAD
+            if (c - 1) in OUT_AT or (c - 2) in OUT_AT:
+                return CV_AFTER_OUT
+            return CV_MAIN
 
         def im(c):
             if c >= NCH or pe_cols(c) == 0:
@@ -135,7 +150,7 @@ def tile_decoder_kernel(tc, x, W, out):
             raw = raw_of[("w", c, 0)]
             grp = grpp.tile([P, A, PACK], BF16, name="grp%d" % c, tag="grp", align_bytes=64)
             grp_of[c] = grp
-            cv = CV_MAIN if pe_cols(c) else CV_HEAD
+            cv = vector_cols(c)
             cs = A - pe_cols(c)
             nc.vector.tensor_copy(
                 out=grp[:, 0:cv, :].rearrange("p (c i) t -> p c t i", i=4),
@@ -176,7 +191,7 @@ def tile_decoder_kernel(tc, x, W, out):
                     acc_of[(i, m, s)] = psum.tile(
                         [P, nw], F32, name="acc%d_%d_%d" % (i, m, s), tag="bk%d" % (2 * m + s)
                     )
-                col = (g * MT + m) * P
+                col = (m * G + g) * P
                 nc.tensor.matmul_mx(
                     out=acc_of[(i, m, s)][:],
                     lhsT=x_codes[:, j, col : col + P].bitcast(FP8X4),
@@ -191,31 +206,37 @@ def tile_decoder_kernel(tc, x, W, out):
             stages = [stagep.tile([P, A], F32, name="st%d_%d" % (i, m)) for m in range(MT)]
             for s, (n0, nw) in enumerate(N_SLICES):
                 nc.scalar.copy(out=stages[0][:, n0 : n0 + nw], in_=acc_of[(i, 0, s)][:])
-                nc.vector.tensor_copy(out=stages[1][:, n0 : n0 + nw], in_=acc_of[(i, 1, s)][:])
+                if i == L - 1:
+                    nc.vector.tensor_copy(out=stages[1][:, n0 : n0 + nw], in_=acc_of[(i, 1, s)][:])
+                else:
+                    nc.scalar.copy(out=stages[1][:, n0 : n0 + nw], in_=acc_of[(i, 1, s)][:])
             for m in range(MT):
                 nc.sync.dma_start(out=out[m * P : (m + 1) * P, i, :], in_=stages[m][:])
 
-        xt(0)
-        xt(1)
-        xe(0)
-        xt(2)
-        xe(1)
-        xq(0)
-        xe(2)
-        xq(1)
-        im(0)
-        rg(0)
-        xq(2)
-        im(1)
-        for c in range(1, NCH):
+        xt(0, 0)
+        xt(0, 1)
+        xe(0, 0)
+        xq(0, 0)
+        xe(0, 1)
+        xq(0, 1)
+        for c in range(PE_FROM):
+            rg(c)
+            if c < len(late_x):
+                xt(*late_x[c])
+            if c >= 1:
+                xq(*late_x[c - 1])
+            if c < len(late_x):
+                qz(c)
+                mm(c)
+                xe(*late_x[c])
+        im(PE_FROM)
+        for c in range(PE_FROM, NCH):
             rg(c)
             qz(c - 1)
             im(c + 1)
-            if c == 5:
-                oe(0)
-            if c == 13:
-                oe(1)
+            if c in OUT_AT:
+                oe(OUT_AT[c])
             mm(c - 1)
         qz(NCH - 1)
         mm(NCH - 1)
-        oe(2)
+        oe(L - 1)

@@ -23,9 +23,10 @@ RAW_BUFS = 20
 N_SLICES = ((0, 512), (512, 256))
 PE_FROM = 5
 PE_COLS = 192
-CV_HEAD = 376
+CV_HEAD = 640
+CV_LAST_HEAD = 504
 CV_MAIN = 312
-CV_AFTER_OUT = 448
+CV_AFTER_OUT = 512
 OUT_AT = {5: 0, 13: 1}
 
 
@@ -125,7 +126,7 @@ def tile_decoder_kernel(tc, x, W, out):
 
         def vector_cols(c):
             if pe_cols(c) == 0:
-                return CV_HEAD
+                return CV_HEAD if c < len(late_x) else CV_LAST_HEAD
             if (c - 1) in OUT_AT or (c - 2) in OUT_AT:
                 return CV_AFTER_OUT
             return CV_MAIN
@@ -216,11 +217,12 @@ def tile_decoder_kernel(tc, x, W, out):
         xt(0, 0)
         xt(0, 1)
         xe(0, 0)
-        xq(0, 0)
         xe(0, 1)
-        xq(0, 1)
+        xq(0, 0)
         for c in range(PE_FROM):
             rg(c)
+            if c == 0:
+                xq(0, 1)
             if c < len(late_x):
                 xt(*late_x[c])
             if c >= 1:

@@ -23,10 +23,10 @@ RAW_BUFS = 20
 N_SLICES = ((0, 512), (512, 256))
 PE_FROM = 5
 PE_COLS = 192
-CV_HEAD = 640
-CV_LAST_HEAD = 504
+CV_HEAD = 456
+CV_LAST_HEAD = 408
 CV_MAIN = 312
-CV_AFTER_OUT = 512
+CV_AFTER_OUT = 464
 OUT_AT = {5: 0, 13: 1}
 
 
@@ -102,10 +102,12 @@ def tile_decoder_kernel(tc, x, W, out):
                 xg_of[j] = xgp.tile([P, MT * G * P * PACK], BF16, name="xg%d" % j, tag="xg", align_bytes=64)
             view = xg_of[j][:].bitcast(F32).rearrange("p (m g b u) -> p m g b u", m=MT, g=G, b=P, u=2)
             for h in range(2):
-                nc.scalar.copy(
-                    out=view[:, m, 2 * h : 2 * h + 2],
-                    in_=xt_of[(j, m, h)][:].rearrange("p g u b -> p g b u"),
-                )
+                dst = view[:, m, 2 * h : 2 * h + 2]
+                src = xt_of[(j, m, h)][:].rearrange("p g u b -> p g b u")
+                if j == 0 and h == 1:
+                    nc.vector.tensor_copy(out=dst, in_=src)
+                else:
+                    nc.scalar.copy(out=dst, in_=src)
             load_next()
 
         def xq(j, m):
@@ -211,14 +213,20 @@ def tile_decoder_kernel(tc, x, W, out):
                     nc.vector.tensor_copy(out=stages[1][:, n0 : n0 + nw], in_=acc_of[(i, 1, s)][:])
                 else:
                     nc.scalar.copy(out=stages[1][:, n0 : n0 + nw], in_=acc_of[(i, 1, s)][:])
-            for m in range(MT):
-                nc.sync.dma_start(out=out[m * P : (m + 1) * P, i, :], in_=stages[m][:])
+                if i == L - 1:
+                    for m in range(MT):
+                        nc.sync.dma_start(
+                            out=out[m * P : (m + 1) * P, i, n0 : n0 + nw], in_=stages[m][:, n0 : n0 + nw]
+                        )
+            if i < L - 1:
+                for m in range(MT):
+                    nc.sync.dma_start(out=out[m * P : (m + 1) * P, i, :], in_=stages[m][:])
 
         xt(0, 0)
         xt(0, 1)
         xe(0, 0)
-        xe(0, 1)
         xq(0, 0)
+        xe(0, 1)
         for c in range(PE_FROM):
             rg(c)
             if c == 0:

@@ -23,11 +23,8 @@ RAW_BUFS = 20
 N_SLICES = ((0, 512), (512, 256))
 PE_FROM = 5
 PE_COLS = 192
-CV_HEAD = 456
-CV_LAST_HEAD = 408
+CV_HEAD = 376
 CV_MAIN = 312
-CV_AFTER_OUT = 464
-OUT_AT = {5: 0, 13: 1}
 
 
 def tile_decoder_kernel(tc, x, W, out):
@@ -47,17 +44,12 @@ def tile_decoder_kernel(tc, x, W, out):
         ident_bf = const.tile([P, P], BF16, name="ident_bf")
         make_identity(nc, ident_bf[:])
 
-        x_codes = const.tile([P, L, MT * G * P], U32, name="x_codes", align_bytes=64)
-        x_scales = const.tile([P, L, MT * G * P], U8, name="x_scales", align_bytes=64)
+        x_codes = const.tile([P, L, G * MT * P], U32, name="x_codes", align_bytes=64)
+        x_scales = const.tile([P, L, G * MT * P], U8, name="x_scales", align_bytes=64)
 
         chunks = [(i, j, g) for i in range(L) for j in range(i + 1) for g in range(G)]
         NCH = len(chunks)
-        late_x = [(1, 0), (1, 1), (2, 0), (2, 1)]
-        items = [("x", 0, 0), ("x", 0, 1)]
-        for c in range(NCH):
-            items.append(("w", c, 0))
-            if c < len(late_x):
-                items.append(("x",) + late_x[c])
+        items = [("x", j, m) for j in range(L) for m in range(MT)] + [("w", c, 0) for c in range(NCH)]
         raw_of = {}
         n_loaded = [0]
 
@@ -84,54 +76,46 @@ def tile_decoder_kernel(tc, x, W, out):
 
         xt_of = {}
         xg_of = {}
-        n_items = [0]
 
-        def xt(j, m):
-            base = 4 + 2 * (n_items[0] % 2)
-            n_items[0] += 1
-            words = raw_of[("x", j, m)][:].bitcast(F32).rearrange("p (g q u) -> p g u q", g=G, q=P, u=2)
-            for h in range(2):
-                bank = psum.tile([P, 2, 2, P], F32, name="xt%d_%d_%d" % (j, m, h), tag="bk%d" % (base + h))
-                for g2 in range(2):
+        def xt(j):
+            base = 0 if j == 1 else 4
+            for g in range(G):
+                bank = psum.tile([P, MT, 2, P], F32, name="xt%d_%d" % (j, g), tag="bk%d" % (base + g))
+                for m in range(MT):
+                    words = raw_of[("x", j, m)][:].bitcast(F32).rearrange(
+                        "p (g q u) -> p g u q", g=G, q=P, u=2
+                    )
                     for u in range(2):
-                        nc.tensor.transpose(bank[:, g2, u, :], words[:, 2 * h + g2, u, :], ident[:])
-                xt_of[(j, m, h)] = bank
+                        nc.tensor.transpose(bank[:, m, u, :], words[:, g, u, :], ident[:])
+                xt_of[(j, g)] = bank
 
-        def xe(j, m):
-            if m == 0:
-                xg_of[j] = xgp.tile([P, MT * G * P * PACK], BF16, name="xg%d" % j, tag="xg", align_bytes=64)
-            view = xg_of[j][:].bitcast(F32).rearrange("p (m g b u) -> p m g b u", m=MT, g=G, b=P, u=2)
-            for h in range(2):
-                dst = view[:, m, 2 * h : 2 * h + 2]
-                src = xt_of[(j, m, h)][:].rearrange("p g u b -> p g b u")
-                if j == 0 and h == 1:
-                    nc.vector.tensor_copy(out=dst, in_=src)
+        def xe(j):
+            xg = xgp.tile([P, G * MT * P * PACK], BF16, name="xg%d" % j, tag="xg", align_bytes=64)
+            xg_of[j] = xg
+            view = xg[:].bitcast(F32).rearrange("p (g m b u) -> p g m b u", g=G, m=MT, b=P, u=2)
+            for g in range(G):
+                src = xt_of[(j, g)][:].rearrange("p m u b -> p m b u")
+                if g == 0:
+                    nc.vector.tensor_copy(out=view[:, g], in_=src)
                 else:
-                    nc.scalar.copy(out=dst, in_=src)
+                    nc.scalar.copy(out=view[:, g], in_=src)
+            load_next()
             load_next()
 
-        def xq(j, m):
-            w = G * P
+        def xq(j):
             nc.vector.quantize_mx(
-                out=x_codes[:, j, m * w : (m + 1) * w].bitcast(FP8X4),
-                scales=x_scales[:, j, m * w : (m + 1) * w],
-                in_=xg_of[j][:, m * w * PACK : (m + 1) * w * PACK],
+                out=x_codes[:, j, :].bitcast(FP8X4), scales=x_scales[:, j, :], in_=xg_of[j][:]
             )
 
         grp_of = {}
         code_of = {}
         acc_of = {}
+        narrow_of = {}
+        st01 = {}
         pg_of = {}
 
         def pe_cols(c):
             return PE_COLS if c >= PE_FROM else 0
-
-        def vector_cols(c):
-            if pe_cols(c) == 0:
-                return CV_HEAD if c < len(late_x) else CV_LAST_HEAD
-            if (c - 1) in OUT_AT or (c - 2) in OUT_AT:
-                return CV_AFTER_OUT
-            return CV_MAIN
 
         def im(c):
             if c >= NCH or pe_cols(c) == 0:
@@ -153,7 +137,7 @@ def tile_decoder_kernel(tc, x, W, out):
             raw = raw_of[("w", c, 0)]
             grp = grpp.tile([P, A, PACK], BF16, name="grp%d" % c, tag="grp", align_bytes=64)
             grp_of[c] = grp
-            cv = vector_cols(c)
+            cv = CV_MAIN if pe_cols(c) else CV_HEAD
             cs = A - pe_cols(c)
             nc.vector.tensor_copy(
                 out=grp[:, 0:cv, :].rearrange("p (c i) t -> p c t i", i=4),
@@ -190,13 +174,16 @@ def tile_decoder_kernel(tc, x, W, out):
                 seq = [(0, 0), (0, 1), (1, 0), (1, 1)]
             for m, s in seq:
                 n0, nw = N_SLICES[s]
-                if first:
-                    acc_of[(i, m, s)] = psum.tile(
-                        [P, nw], F32, name="acc%d_%d_%d" % (i, m, s), tag="bk%d" % (2 * m + s)
-                    )
-                col = (m * G + g) * P
+                if first and s == 1 and i == 0:
+                    narrow_of[m] = psum.tile([P, 2, nw], F32, name="accn_%d" % m, tag="bk%d" % (2 * m + s))
+                if first and s == 1 and i < 2:
+                    acc_of[(i, m, s)] = narrow_of[m][:, i, :]
+                elif first:
+                    bank = psum.tile([P, nw], F32, name="acc%d_%d_%d" % (i, m, s), tag="bk%d" % (2 * m + s))
+                    acc_of[(i, m, s)] = bank[:]
+                col = (g * MT + m) * P
                 nc.tensor.matmul_mx(
-                    out=acc_of[(i, m, s)][:],
+                    out=acc_of[(i, m, s)],
                     lhsT=x_codes[:, j, col : col + P].bitcast(FP8X4),
                     lhsT_scale=x_scales[:, j, col : col + P],
                     rhs=codes[:, n0 : n0 + nw].bitcast(FP8X4),
@@ -205,48 +192,56 @@ def tile_decoder_kernel(tc, x, W, out):
                     stop=last,
                 )
 
+        def copy_out(m, dst, src):
+            if m == 0:
+                nc.scalar.copy(out=dst, in_=src)
+            else:
+                nc.vector.tensor_copy(out=dst, in_=src)
+
         def oe(i):
-            stages = [stagep.tile([P, A], F32, name="st%d_%d" % (i, m)) for m in range(MT)]
-            for s, (n0, nw) in enumerate(N_SLICES):
-                nc.scalar.copy(out=stages[0][:, n0 : n0 + nw], in_=acc_of[(i, 0, s)][:])
-                if i == L - 1:
-                    nc.vector.tensor_copy(out=stages[1][:, n0 : n0 + nw], in_=acc_of[(i, 1, s)][:])
-                else:
-                    nc.scalar.copy(out=stages[1][:, n0 : n0 + nw], in_=acc_of[(i, 1, s)][:])
-                if i == L - 1:
+            n1, w1 = N_SLICES[1]
+            if i == 0:
+                for m in range(MT):
+                    st01[m] = stagep.tile([P, 2, A], F32, name="st01_%d" % m)
+            if i < 2:
+                for m in range(MT):
+                    copy_out(m, st01[m][:, i, 0:n1], acc_of[(i, m, 0)])
+            if i == 1:
+                for m in range(MT):
+                    copy_out(m, st01[m][:, :, n1 : n1 + w1], narrow_of[m][:])
+                for m in range(MT):
+                    nc.sync.dma_start(out=out[m * P : (m + 1) * P, 0:2, :], in_=st01[m][:])
+            if i == 2:
+                stages = [stagep.tile([P, A], F32, name="st2_%d" % m) for m in range(MT)]
+                for s, (n0, nw) in enumerate(N_SLICES):
+                    for m in range(MT):
+                        copy_out(m, stages[m][:, n0 : n0 + nw], acc_of[(i, m, s)])
                     for m in range(MT):
                         nc.sync.dma_start(
                             out=out[m * P : (m + 1) * P, i, n0 : n0 + nw], in_=stages[m][:, n0 : n0 + nw]
                         )
-            if i < L - 1:
-                for m in range(MT):
-                    nc.sync.dma_start(out=out[m * P : (m + 1) * P, i, :], in_=stages[m][:])
 
-        xt(0, 0)
-        xt(0, 1)
-        xe(0, 0)
-        xq(0, 0)
-        xe(0, 1)
-        for c in range(PE_FROM):
-            rg(c)
-            if c == 0:
-                xq(0, 1)
-            if c < len(late_x):
-                xt(*late_x[c])
-            if c >= 1:
-                xq(*late_x[c - 1])
-            if c < len(late_x):
-                qz(c)
-                mm(c)
-                xe(*late_x[c])
-        im(PE_FROM)
-        for c in range(PE_FROM, NCH):
+        xt(0)
+        xt(1)
+        xe(0)
+        xt(2)
+        xe(1)
+        xq(0)
+        xe(2)
+        xq(1)
+        im(0)
+        rg(0)
+        xq(2)
+        im(1)
+        for c in range(1, NCH):
             rg(c)
             qz(c - 1)
             im(c + 1)
-            if c in OUT_AT:
-                oe(OUT_AT[c])
+            if c == 5:
+                oe(0)
+            if c == 13:
+                oe(1)
             mm(c - 1)
         qz(NCH - 1)
         mm(NCH - 1)
-        oe(L - 1)
+        oe(2)

from contextlib import ExitStack

import concourse.mybir as mybir
from concourse.masks import make_identity

FP8X4 = mybir.dt.float8_e4m3fn_x4
BF16 = mybir.dt.bfloat16
F32 = mybir.dt.float32
U32 = mybir.dt.uint32
U8 = mybir.dt.uint8

P = 128
B, L, F, A = 256, 3, 2048, 768
PACK = 4
K_PASS = P * PACK
G = F // K_PASS
MT = B // P

FLOPS = 2 * B * F * A * 6
BYTES = B * L * F * 2 + 6 * F * A * 2 + B * L * A * 4

RAW_BUFS = 20
N_SLICES = ((0, 512), (512, 256))
PE_FROM = 5
PE_COLS = 192
CV_HEAD = 376
CV_MAIN = 312


def tile_decoder_kernel(tc, x, W, out):
    nc = tc.nc
    with ExitStack() as ctx:
        const = ctx.enter_context(tc.tile_pool(name="const", bufs=1))
        rawp = ctx.enter_context(tc.tile_pool(name="rawp", bufs=RAW_BUFS))
        xgp = ctx.enter_context(tc.tile_pool(name="xgp", bufs=3))
        grpp = ctx.enter_context(tc.tile_pool(name="grpp", bufs=4))
        codep = ctx.enter_context(tc.tile_pool(name="codep", bufs=6))
        stagep = ctx.enter_context(tc.tile_pool(name="stagep", bufs=1))
        psum = ctx.enter_context(tc.psum_pool(name="psum", bufs=1))
        ctx.enter_context(tc.manual_schedule())

        ident = const.tile([P, P], F32, name="ident")
        make_identity(nc, ident[:])
        ident_bf = const.tile([P, P], BF16, name="ident_bf")
        make_identity(nc, ident_bf[:])

        x_codes = const.tile([P, L, G * MT * P], U32, name="x_codes", align_bytes=64)
        x_scales = const.tile([P, L, G * MT * P], U8, name="x_scales", align_bytes=64)

        chunks = [(i, j, g) for i in range(L) for j in range(i + 1) for g in range(G)]
        NCH = len(chunks)
        items = [("x", j, m) for j in range(L) for m in range(MT)] + [("w", c, 0) for c in range(NCH)]
        raw_of = {}
        n_loaded = [0]

        def load_next():
            n = n_loaded[0]
            if n >= len(items):
                return
            n_loaded[0] = n + 1
            kind, a0, a1 = items[n]
            if kind == "x":
                t = rawp.tile([P, F], BF16, name="xraw%d_%d" % (a0, a1), tag="raw", align_bytes=64)
                nc.sync.dma_start(out=t[:], in_=x[a1 * P : (a1 + 1) * P, a0, :])
            else:
                i, j, g = chunks[a0]
                t = rawp.tile([P, PACK, A], BF16, name="wraw%d" % a0, tag="raw", align_bytes=64)
                nc.sync.dma_start(
                    out=t[:],
                    in_=W[i, j, g * K_PASS : (g + 1) * K_PASS, :].rearrange("(p t) a -> p t a", t=PACK),
                )
            raw_of[(kind, a0, a1)] = t

        for n in range(RAW_BUFS):
            load_next()

        xt_of = {}
        xg_of = {}

        def xt(j):
            base = 0 if j == 1 else 4
            for g in range(G):
                bank = psum.tile([P, MT, 2, P], F32, name="xt%d_%d" % (j, g), tag="bk%d" % (base + g))
                for m in range(MT):
                    words = raw_of[("x", j, m)][:].bitcast(F32).rearrange(
                        "p (g q u) -> p g u q", g=G, q=P, u=2
                    )
                    for u in range(2):
                        nc.tensor.transpose(bank[:, m, u, :], words[:, g, u, :], ident[:])
                xt_of[(j, g)] = bank

        def xe(j):
            xg = xgp.tile([P, G * MT * P * PACK], BF16, name="xg%d" % j, tag="xg", align_bytes=64)
            xg_of[j] = xg
            view = xg[:].bitcast(F32).rearrange("p (g m b u) -> p g m b u", g=G, m=MT, b=P, u=2)
            for g in range(G):
                src = xt_of[(j, g)][:].rearrange("p m u b -> p m b u")
                if g == 0:
                    nc.vector.tensor_copy(out=view[:, g], in_=src)
                else:
                    nc.scalar.copy(out=view[:, g], in_=src)
            load_next()
            load_next()

        def xq(j):
            nc.vector.quantize_mx(
                out=x_codes[:, j, :].bitcast(FP8X4), scales=x_scales[:, j, :], in_=xg_of[j][:]
            )

        grp_of = {}
        code_of = {}
        acc_of = {}
        narrow_of = {}
        st01 = {}
        pg_of = {}

        def pe_cols(c):
            return PE_COLS if c >= PE_FROM else 0

        def im(c):
            if c >= NCH or pe_cols(c) == 0:
                return
            raw = raw_of[("w", c, 0)]
            pg = psum.tile([P, PE_COLS * PACK], BF16, name="pg%d" % c, tag="bk%d" % (4 + c % 4))
            pg_of[c] = pg
            a0 = A - PE_COLS
            for o0, ow in ((0, 128), (128, 64)):
                nc.tensor.matmul(
                    out=pg[:, o0 * PACK : (o0 + ow) * PACK].rearrange("p (a t) -> p t a", t=PACK),
                    lhsT=ident_bf[:],
                    rhs=raw[:, :, a0 + o0 : a0 + o0 + ow],
                    start=True,
                    stop=True,
                )

        def rg(c):
            raw = raw_of[("w", c, 0)]
            grp = grpp.tile([P, A, PACK], BF16, name="grp%d" % c, tag="grp", align_bytes=64)
            grp_of[c] = grp
            cv = CV_MAIN if pe_cols(c) else CV_HEAD
            cs = A - pe_cols(c)
            nc.vector.tensor_copy(
                out=grp[:, 0:cv, :].rearrange("p (c i) t -> p c t i", i=4),
                in_=raw[:, :, 0:cv].rearrange("p t (c i) -> p c t i", i=4),
            )
            nc.scalar.copy(
                out=grp[:, cv:cs, :].rearrange("p (c i) t -> p c t i", i=4),
                in_=raw[:, :, cv:cs].rearrange("p t (c i) -> p c t i", i=4),
            )
            if pe_cols(c):
                nc.scalar.copy(out=grp[:, cs:A, :].rearrange("p a t -> p (a t)"), in_=pg_of[c][:])
            load_next()

        def qz(c):
            codes = codep.tile([P, A], U32, name="wc%d" % c, tag="wc", align_bytes=64)
            scales = codep.tile([P, A], U8, name="ws%d" % c, tag="ws", align_bytes=64)
            code_of[c] = (codes, scales)
            flat = grp_of[c][:].rearrange("p a t -> p (a t)")
            for n0, nw in N_SLICES:
                nc.vector.quantize_mx(
                    out=codes[:, n0 : n0 + nw].bitcast(FP8X4),
                    scales=scales[:, n0 : n0 + nw],
                    in_=flat[:, n0 * PACK : (n0 + nw) * PACK],
                )

        def mm(c):
            i, j, g = chunks[c]
            codes, scales = code_of[c]
            first = j == 0 and g == 0
            last = j == i and g == G - 1
            if c == NCH - 1:
                seq = [(0, 0), (1, 0), (0, 1), (1, 1)]
            else:
                seq = [(0, 0), (0, 1), (1, 0), (1, 1)]
            for m, s in seq:
                n0, nw = N_SLICES[s]
                if first and s == 1 and i == 0:
                    narrow_of[m] = psum.tile([P, 2, nw], F32, name="accn_%d" % m, tag="bk%d" % (2 * m + s))
                if first and s == 1 and i < 2:
                    acc_of[(i, m, s)] = narrow_of[m][:, i, :]
                elif first:
                    bank = psum.tile([P, nw], F32, name="acc%d_%d_%d" % (i, m, s), tag="bk%d" % (2 * m + s))
                    acc_of[(i, m, s)] = bank[:]
                col = (g * MT + m) * P
                nc.tensor.matmul_mx(
                    out=acc_of[(i, m, s)],
                    lhsT=x_codes[:, j, col : col + P].bitcast(FP8X4),
                    lhsT_scale=x_scales[:, j, col : col + P],
                    rhs=codes[:, n0 : n0 + nw].bitcast(FP8X4),
                    rhs_scale=scales[:, n0 : n0 + nw],
                    start=first,
                    stop=last,
                )

        def copy_out(m, dst, src):
            if m == 0:
                nc.scalar.copy(out=dst, in_=src)
            else:
                nc.vector.tensor_copy(out=dst, in_=src)

        def oe(i):
            n1, w1 = N_SLICES[1]
            if i == 0:
                for m in range(MT):
                    st01[m] = stagep.tile([P, 2, A], F32, name="st01_%d" % m)
            if i < 2:
                for m in range(MT):
                    copy_out(m, st01[m][:, i, 0:n1], acc_of[(i, m, 0)])
            if i == 1:
                for m in range(MT):
                    copy_out(m, st01[m][:, :, n1 : n1 + w1], narrow_of[m][:])
                for m in range(MT):
                    nc.sync.dma_start(out=out[m * P : (m + 1) * P, 0:2, :], in_=st01[m][:])
            if i == 2:
                stages = [stagep.tile([P, A], F32, name="st2_%d" % m) for m in range(MT)]
                for s, (n0, nw) in enumerate(N_SLICES):
                    for m in range(MT):
                        copy_out(m, stages[m][:, n0 : n0 + nw], acc_of[(i, m, s)])
                    for m in range(MT):
                        nc.sync.dma_start(
                            out=out[m * P : (m + 1) * P, i, n0 : n0 + nw], in_=stages[m][:, n0 : n0 + nw]
                        )

        xt(0)
        xt(1)
        xe(0)
        xt(2)
        xe(1)
        xq(0)
        xe(2)
        xq(1)
        im(0)
        rg(0)
        xq(2)
        im(1)
        for c in range(1, NCH):
            rg(c)
            qz(c - 1)
            im(c + 1)
            if c == 5:
                oe(0)
            if c == 13:
                oe(1)
            mm(c - 1)
        qz(NCH - 1)
        mm(NCH - 1)
        oe(2)
